import numpy as np
import ml_dtypes

BF16 = ml_dtypes.bfloat16


def bf(x):
    return np.asarray(x, np.float32).astype(BF16)


def f32(x):
    return np.asarray(x, np.float32)


def f64(x):
    return np.asarray(x).astype(np.float64)


def striped(idx):
    return np.tile(idx.reshape(-1, 16).T, (8, 1))


C, S, K, H, N = 1024, 256, 8, 128, 1024


def setup_inputs():
    return {"table": f32(np.random.standard_normal((C, S))), "src": bf(np.random.standard_normal((C, H))), "v": bf(np.random.standard_normal((C, C)) / np.sqrt(C)), "b": f32(0.1 * np.random.standard_normal((C, 1))), "att": bf(0.1 * np.random.standard_normal((C, 1))), "offs": striped(np.concatenate([np.random.permutation(S)[:H] for _ in range(K)]))}


def reference(table, src, v, b, att, offs):
    idx = offs[:16].T.reshape(-1)
    u = f64(v).T @ f64(src) + f64(b)
    t = f64(table)[:, idx].reshape(C, K, H)
    h = np.tanh(t + u[:, None, :])
    s = (f64(att)[:, :, None] * h).sum(axis=0)
    e = np.exp(s)
    a = e / (e.sum(axis=0)[None, :] + (S - K))
    return f64(src) + (a[None, :, :] * t).sum(axis=1)

@@ -1,0 +1,130 @@
+import concourse.mybir as mybir
+from concourse.masks import make_identity
+
+F32 = mybir.dt.float32
+BF16 = mybir.dt.bfloat16
+U16 = mybir.dt.uint16
+ALU = mybir.AluOpType
+ACT = mybir.ActivationFunctionType
+AXIS_X = mybir.AxisListType.X
+
+P = 128
+C, S, K, H = 1024, 256, 8, 128
+NB = C // P
+OFFS_COLS = H // 16
+BANK = 512
+SLOTS_IN_BANK = BANK // H
+NBANKS = K // SLOTS_IN_BANK
+UNLISTED = float(S - K)
+
+FLOPS = 2 * C * C * H + 2 * C * K * H
+
+
+def tile_attributeembeddinglayer_kernel(tc, table, src, v, b, att, offs, out):
+    nc = tc.nc
+    with (
+        tc.tile_pool(name="held", bufs=1) as held,
+        tc.tile_pool(name="work", bufs=4) as work,
+        tc.psum_pool(name="block_psum", bufs=2) as block_psum,
+        tc.psum_pool(name="logit_psum", bufs=1) as logit_psum,
+    ):
+        offsets = held.tile([P, K * OFFS_COLS], U16, name="offsets")
+        nc.sync.dma_start(offsets[:], offs)
+        src_sb = held.tile([P, NB, H], BF16, name="src_sb")
+        nc.sync.dma_start(src_sb[:], src.rearrange("(n p) i -> p n i", p=P))
+        b_col = held.tile([P, NB], F32, name="b_col")
+        att_col = held.tile([P, NB], BF16, name="att_col")
+        with nc.allow_non_contiguous_dma(reason="one element to a partition: 1024 small pieces, once"):
+            nc.gpsimd.dma_start(b_col[:], b.rearrange("(n p) o -> p (n o)", p=P))
+            nc.gpsimd.dma_start(att_col[:], att.rearrange("(n p) o -> p (n o)", p=P))
+        v_sb = []
+        table_sb = []
+        for n in range(NB):
+            v_rows = held.tile([P, C], BF16, name=f"v{n}")
+            nc.sync.dma_start(v_rows[:], v[n * P : (n + 1) * P, :])
+            v_sb.append(v_rows)
+            table_rows = held.tile([P, S], F32, name=f"table{n}")
+            nc.scalar.dma_start(table_rows[:], table[n * P : (n + 1) * P, :])
+            table_sb.append(table_rows)
+
+        ident_f32 = held.tile([P, P], F32, name="ident_f32")
+        make_identity(nc, ident_f32[:])
+        ident_bf = held.tile([P, P], BF16, name="ident_bf")
+        make_identity(nc, ident_bf[:])
+        att_rep = held.tile([P, NB, P], BF16, name="att_rep")
+        nc.vector.tensor_copy(att_rep[:], att_col[:].unsqueeze(2).to_broadcast([P, NB, P]))
+
+        u_sb = []
+        for cb in range(NB):
+            u_ps = block_psum.tile([P, H], F32, name="u_ps")
+            for eb in range(NB):
+                nc.tensor.matmul(
+                    u_ps[:],
+                    lhsT=v_sb[eb][:, cb * P : (cb + 1) * P],
+                    rhs=src_sb[:, eb, :],
+                    start=(eb == 0),
+                    stop=(eb == NB - 1),
+                )
+            u_block = held.tile([P, H], F32, name=f"u{cb}")
+            nc.scalar.activation(u_block[:], u_ps[:], ACT.Identity, bias=b_col[:, cb : cb + 1])
+            u_sb.append(u_block)
+
+        s_bank = [logit_psum.tile([P, BANK], F32, name=f"s_bank{j}") for j in range(NBANKS)]
+        for cb in range(NB):
+            h = work.tile([P, K * H], BF16, name="h")
+            for k in range(K):
+                z = work.tile([P, H], F32, name="z")
+                picked = table_sb[cb][:].indirect(offsets[:, k * OFFS_COLS : (k + 1) * OFFS_COLS])
+                nc.vector.tensor_tensor(z[:], picked, u_sb[cb][:], ALU.add)
+                nc.scalar.activation(h[:, k * H : (k + 1) * H], z[:], ACT.Tanh)
+            for j in range(NBANKS):
+                nc.tensor.matmul(
+                    s_bank[j][:],
+                    lhsT=att_rep[:, cb, :],
+                    rhs=h[:, j * BANK : (j + 1) * BANK],
+                    start=(cb == 0),
+                    stop=(cb == NB - 1),
+                )
+
+        top = [held.tile([P, H], F32, name=f"top{j}") for j in range(NBANKS)]
+        for j in range(NBANKS):
+            nc.vector.tensor_reduce(
+                out=top[j][:],
+                in_=s_bank[j][:].rearrange("p (k i) -> p i k", k=SLOTS_IN_BANK),
+                axis=AXIS_X,
+                op=ALU.max,
+            )
+        shift = held.tile([P, H], F32, name="shift")
+        nc.vector.scalar_tensor_tensor(shift[:], top[0][:], 0.0, top[1][:], op0=ALU.max, op1=ALU.max)
+        centred = held.tile([P, K, H], F32, name="centred")
+        for j in range(NBANKS):
+            nc.vector.tensor_tensor(
+                centred[:, j * SLOTS_IN_BANK : (j + 1) * SLOTS_IN_BANK, :],
+                s_bank[j][:].rearrange("p (k i) -> p k i", k=SLOTS_IN_BANK),
+                shift[:].unsqueeze(1).to_broadcast([P, SLOTS_IN_BANK, H]),
+                ALU.subtract,
+            )
+        e = held.tile([P, K, H], F32, name="e")
+        nc.scalar.activation(e[:], centred[:], ACT.Exp)
+        e_zero = held.tile([P, H], F32, name="e_zero")
+        nc.scalar.activation(e_zero[:], shift[:], ACT.Exp, scale=-1.0)
+        e_sum = held.tile([P, H], F32, name="e_sum")
+        nc.vector.tensor_reduce(out=e_sum[:], in_=e[:].rearrange("p k i -> p i k"), axis=AXIS_X, op=ALU.add)
+        denom = held.tile([P, H], F32, name="denom")
+        nc.vector.scalar_tensor_tensor(denom[:], e_zero[:], UNLISTED, e_sum[:], op0=ALU.mult, op1=ALU.add)
+        recip = held.tile([P, H], F32, name="recip")
+        nc.vector.reciprocal(recip[:], denom[:])
+        a = held.tile([P, K, H], F32, name="a")
+        nc.vector.tensor_tensor(a[:], e[:], recip[:].unsqueeze(1).to_broadcast([P, K, H]), ALU.mult)
+
+        for cb in range(NB):
+            acc = block_psum.tile([P, H], F32, name="acc")
+            nc.tensor.matmul(acc[:], lhsT=ident_bf[:], rhs=src_sb[:, cb, :], start=True, stop=False)
+            for k in range(K):
+                prod = work.tile([P, H], F32, name="prod")
+                picked = table_sb[cb][:].indirect(offsets[:, k * OFFS_COLS : (k + 1) * OFFS_COLS])
+                nc.vector.tensor_tensor(prod[:], picked, a[:, k, :], ALU.mult)
+                nc.tensor.matmul(acc[:], lhsT=ident_f32[:], rhs=prod[:], start=False, stop=(k == K - 1))
+            res = work.tile([P, H], F32, name="res")
+            nc.scalar.copy(res[:], acc[:])
+            nc.sync.dma_start(out[cb * P : (cb + 1) * P, :], res[:])

@@ -11,7 +11,10 @@ AXIS_X = mybir.AxisListType.X
 P = 128
 C, S, K, H = 1024, 256, 8, 128
 NB = C // P
-OFFS_COLS = H // 16
+PIECE_SLOTS = 2
+PIECE = PIECE_SLOTS * H
+NPIECES = K // PIECE_SLOTS
+OFFS_COLS = PIECE // 16
 BANK = 512
 SLOTS_IN_BANK = BANK // H
 NBANKS = K // SLOTS_IN_BANK
@@ -28,7 +31,7 @@ def tile_attributeembeddinglayer_kernel(tc, table, src, v, b, att, offs, out):
         tc.psum_pool(name="block_psum", bufs=2) as block_psum,
         tc.psum_pool(name="logit_psum", bufs=1) as logit_psum,
     ):
-        offsets = held.tile([P, K * OFFS_COLS], U16, name="offsets")
+        offsets = held.tile([P, NPIECES * OFFS_COLS], U16, name="offsets")
         nc.sync.dma_start(offsets[:], offs)
         src_sb = held.tile([P, NB, H], BF16, name="src_sb")
         nc.sync.dma_start(src_sb[:], src.rearrange("(n p) i -> p n i", p=P))
@@ -65,18 +68,21 @@ def tile_attributeembeddinglayer_kernel(tc, table, src, v, b, att, offs, out):
                     start=(eb == 0),
                     stop=(eb == NB - 1),
                 )
-            u_block = held.tile([P, H], F32, name=f"u{cb}")
-            nc.scalar.activation(u_block[:], u_ps[:], ACT.Identity, bias=b_col[:, cb : cb + 1])
+            u_block = held.tile([P, PIECE], F32, name=f"u{cb}")
+            for t in range(PIECE_SLOTS):
+                nc.scalar.activation(
+                    u_block[:, t * H : (t + 1) * H], u_ps[:], ACT.Identity, bias=b_col[:, cb : cb + 1]
+                )
             u_sb.append(u_block)
 
         s_bank = [logit_psum.tile([P, BANK], F32, name=f"s_bank{j}") for j in range(NBANKS)]
         for cb in range(NB):
             h = work.tile([P, K * H], BF16, name="h")
-            for k in range(K):
-                z = work.tile([P, H], F32, name="z")
-                picked = table_sb[cb][:].indirect(offsets[:, k * OFFS_COLS : (k + 1) * OFFS_COLS])
+            for q in range(NPIECES):
+                z = work.tile([P, PIECE], F32, name="z")
+                picked = table_sb[cb][:].indirect(offsets[:, q * OFFS_COLS : (q + 1) * OFFS_COLS])
                 nc.vector.tensor_tensor(z[:], picked, u_sb[cb][:], ALU.add)
-                nc.scalar.activation(h[:, k * H : (k + 1) * H], z[:], ACT.Tanh)
+                nc.scalar.activation(h[:, q * PIECE : (q + 1) * PIECE], z[:], ACT.Tanh)
             for j in range(NBANKS):
                 nc.tensor.matmul(
                     s_bank[j][:],
@@ -114,17 +120,26 @@ def tile_attributeembeddinglayer_kernel(tc, table, src, v, b, att, offs, out):
         nc.vector.scalar_tensor_tensor(denom[:], e_zero[:], UNLISTED, e_sum[:], op0=ALU.mult, op1=ALU.add)
         recip = held.tile([P, H], F32, name="recip")
         nc.vector.reciprocal(recip[:], denom[:])
-        a = held.tile([P, K, H], F32, name="a")
-        nc.vector.tensor_tensor(a[:], e[:], recip[:].unsqueeze(1).to_broadcast([P, K, H]), ALU.mult)
+        a = held.tile([P, K * H], F32, name="a")
+        nc.vector.tensor_tensor(
+            a[:].rearrange("p (k i) -> p k i", k=K), e[:], recip[:].unsqueeze(1).to_broadcast([P, K, H]), ALU.mult
+        )
 
         for cb in range(NB):
             acc = block_psum.tile([P, H], F32, name="acc")
             nc.tensor.matmul(acc[:], lhsT=ident_bf[:], rhs=src_sb[:, cb, :], start=True, stop=False)
-            for k in range(K):
-                prod = work.tile([P, H], F32, name="prod")
-                picked = table_sb[cb][:].indirect(offsets[:, k * OFFS_COLS : (k + 1) * OFFS_COLS])
-                nc.vector.tensor_tensor(prod[:], picked, a[:, k, :], ALU.mult)
-                nc.tensor.matmul(acc[:], lhsT=ident_f32[:], rhs=prod[:], start=False, stop=(k == K - 1))
+            for q in range(NPIECES):
+                prod = work.tile([P, PIECE], F32, name="prod")
+                picked = table_sb[cb][:].indirect(offsets[:, q * OFFS_COLS : (q + 1) * OFFS_COLS])
+                nc.vector.tensor_tensor(prod[:], picked, a[:, q * PIECE : (q + 1) * PIECE], ALU.mult)
+                for t in range(PIECE_SLOTS):
+                    nc.tensor.matmul(
+                        acc[:],
+                        lhsT=ident_f32[:],
+                        rhs=prod[:, t * H : (t + 1) * H],
+                        start=False,
+                        stop=(q == NPIECES - 1 and t == PIECE_SLOTS - 1),
+                    )
             res = work.tile([P, H], F32, name="res")
             nc.scalar.copy(res[:], acc[:])
             nc.sync.dma_start(out[cb * P : (cb + 1) * P, :], res[:])

@@ -54,6 +54,10 @@ def tile_attributeembeddinglayer_kernel(tc, table, src, v, b, att, offs, out):
         make_identity(nc, ident_f32[:])
         ident_bf = held.tile([P, P], BF16, name="ident_bf")
         make_identity(nc, ident_bf[:])
+        ones_f32 = held.tile([P, P], F32, name="ones_f32")
+        nc.gpsimd.memset(ones_f32[:], 1.0)
+        ones_bf = held.tile([P, P], BF16, name="ones_bf")
+        nc.gpsimd.memset(ones_bf[:], 1.0)
         att_rep = held.tile([P, NB, P], BF16, name="att_rep")
         nc.vector.tensor_copy(att_rep[:], att_col[:].unsqueeze(2).to_broadcast([P, NB, P]))
 
@@ -76,6 +80,7 @@ def tile_attributeembeddinglayer_kernel(tc, table, src, v, b, att, offs, out):
             u_sb.append(u_block)
 
         s_bank = [logit_psum.tile([P, BANK], F32, name=f"s_bank{j}") for j in range(NBANKS)]
+        s_node = logit_psum.tile([P, K], F32, name="s_node")
         for cb in range(NB):
             h = work.tile([P, K * H], BF16, name="h")
             for q in range(NPIECES):
@@ -83,52 +88,69 @@ def tile_attributeembeddinglayer_kernel(tc, table, src, v, b, att, offs, out):
                 picked = table_sb[cb][:].indirect(offsets[:, q * OFFS_COLS : (q + 1) * OFFS_COLS])
                 nc.vector.tensor_tensor(z[:], picked, u_sb[cb][:], ALU.add)
                 nc.scalar.activation(h[:, q * PIECE : (q + 1) * PIECE], z[:], ACT.Tanh)
-            for j in range(NBANKS):
+                for k in range(q * PIECE_SLOTS, (q + 1) * PIECE_SLOTS):
+                    nc.tensor.matmul(
+                        s_node[:, k : k + 1],
+                        lhsT=h[:, k * H : (k + 1) * H],
+                        rhs=att_col[:, cb : cb + 1],
+                        start=(cb == 0 and k == 0),
+                        stop=(cb == NB - 1 and k == K - 1),
+                    )
+                bank, in_bank = divmod(q * PIECE, BANK)
                 nc.tensor.matmul(
-                    s_bank[j][:],
+                    s_bank[bank][:, in_bank : in_bank + PIECE],
                     lhsT=att_rep[:, cb, :],
-                    rhs=h[:, j * BANK : (j + 1) * BANK],
-                    start=(cb == 0),
-                    stop=(cb == NB - 1),
+                    rhs=h[:, q * PIECE : (q + 1) * PIECE],
+                    start=(cb == 0 and in_bank == 0),
+                    stop=False,
                 )
 
-        top = [held.tile([P, H], F32, name=f"top{j}") for j in range(NBANKS)]
+        neg_top = held.tile([P, 1], F32, name="neg_top")
+        nc.vector.tensor_reduce(out=neg_top[:], in_=s_node[:], axis=AXIS_X, op=ALU.max, negate=True)
+        neg_shift_diag = held.tile([P, P], BF16, name="neg_shift_diag")
+        nc.vector.tensor_scalar(neg_shift_diag[:], ident_bf[:], neg_top[:, 0:1], 0.0, op0=ALU.mult, op1=ALU.min)
+        neg_shift = held.tile([P, 1], BF16, name="neg_shift")
+        nc.vector.tensor_scalar_min(neg_shift[:], neg_top[:], 0.0)
         for j in range(NBANKS):
-            nc.vector.tensor_reduce(
-                out=top[j][:],
-                in_=s_bank[j][:].rearrange("p (k i) -> p i k", k=SLOTS_IN_BANK),
-                axis=AXIS_X,
-                op=ALU.max,
-            )
-        shift = held.tile([P, H], F32, name="shift")
-        nc.vector.scalar_tensor_tensor(shift[:], top[0][:], 0.0, top[1][:], op0=ALU.max, op1=ALU.max)
-        centred = held.tile([P, K, H], F32, name="centred")
-        for j in range(NBANKS):
-            nc.vector.tensor_tensor(
-                centred[:, j * SLOTS_IN_BANK : (j + 1) * SLOTS_IN_BANK, :],
+            nc.tensor.matmul(
                 s_bank[j][:].rearrange("p (k i) -> p k i", k=SLOTS_IN_BANK),
-                shift[:].unsqueeze(1).to_broadcast([P, SLOTS_IN_BANK, H]),
-                ALU.subtract,
+                lhsT=ones_bf[:],
+                rhs=neg_shift_diag[:].unsqueeze(1).to_broadcast([P, SLOTS_IN_BANK, H]),
+                start=False,
+                stop=True,
             )
-        e = held.tile([P, K, H], F32, name="e")
-        nc.scalar.activation(e[:], centred[:], ACT.Exp)
-        e_zero = held.tile([P, H], F32, name="e_zero")
-        nc.scalar.activation(e_zero[:], shift[:], ACT.Exp, scale=-1.0)
-        e_sum = held.tile([P, H], F32, name="e_sum")
-        nc.vector.tensor_reduce(out=e_sum[:], in_=e[:].rearrange("p k i -> p i k"), axis=AXIS_X, op=ALU.add)
-        denom = held.tile([P, H], F32, name="denom")
-        nc.vector.scalar_tensor_tensor(denom[:], e_zero[:], UNLISTED, e_sum[:], op0=ALU.mult, op1=ALU.add)
-        recip = held.tile([P, H], F32, name="recip")
+        e_node = held.tile([P, K], F32, name="e_node")
+        e_node_sum = held.tile([P, 1], F32, name="e_node_sum")
+        nc.scalar.activation(e_node[:], s_node[:], ACT.Exp, bias=neg_shift[:, 0:1], accum_out=e_node_sum[:])
+        e_zero = held.tile([P, 1], F32, name="e_zero")
+        nc.scalar.activation(e_zero[:], neg_shift[:], ACT.Exp)
+        denom = held.tile([P, 1], F32, name="denom")
+        nc.vector.scalar_tensor_tensor(denom[:], e_zero[:], UNLISTED, e_node_sum[:], op0=ALU.mult, op1=ALU.add)
+        recip = held.tile([P, 1], F32, name="recip")
         nc.vector.reciprocal(recip[:], denom[:])
+        recip_diag = held.tile([P, P], F32, name="recip_diag")
+        nc.vector.tensor_scalar_mul(recip_diag[:], ident_f32[:], recip[:, 0:1])
+        recip_rep = logit_psum.tile([P, H], F32, name="recip_rep")
+        nc.tensor.matmul(recip_rep[:], lhsT=ones_f32[:], rhs=recip_diag[:], start=True, stop=True)
+        e = held.tile([P, K * H], F32, name="e")
         a = held.tile([P, K * H], F32, name="a")
-        nc.vector.tensor_tensor(
-            a[:].rearrange("p (k i) -> p k i", k=K), e[:], recip[:].unsqueeze(1).to_broadcast([P, K, H]), ALU.mult
-        )
+        for q in range(NPIECES):
+            bank, in_bank = divmod(q * PIECE, BANK)
+            nc.scalar.activation(
+                e[:, q * PIECE : (q + 1) * PIECE], s_bank[bank][:, in_bank : in_bank + PIECE], ACT.Exp
+            )
 
         for cb in range(NB):
             acc = block_psum.tile([P, H], F32, name="acc")
             nc.tensor.matmul(acc[:], lhsT=ident_bf[:], rhs=src_sb[:, cb, :], start=True, stop=False)
             for q in range(NPIECES):
+                if cb == 0:
+                    nc.vector.tensor_tensor(
+                        a[:, q * PIECE : (q + 1) * PIECE].rearrange("p (t i) -> p t i", t=PIECE_SLOTS),
+                        e[:, q * PIECE : (q + 1) * PIECE].rearrange("p (t i) -> p t i", t=PIECE_SLOTS),
+                        recip_rep[:].unsqueeze(1).to_broadcast([P, PIECE_SLOTS, H]),
+                        ALU.mult,
+                    )
                 prod = work.tile([P, PIECE], F32, name="prod")
                 picked = table_sb[cb][:].indirect(offsets[:, q * OFFS_COLS : (q + 1) * OFFS_COLS])
                 nc.vector.tensor_tensor(prod[:], picked, a[:, q * PIECE : (q + 1) * PIECE], ALU.mult)

@@ -15,6 +15,7 @@ PIECE_SLOTS = 2
 PIECE = PIECE_SLOTS * H
 NPIECES = K // PIECE_SLOTS
 OFFS_COLS = PIECE // 16
+V_BLOCKS = 2
 BANK = 512
 SLOTS_IN_BANK = BANK // H
 NBANKS = K // SLOTS_IN_BANK
@@ -33,22 +34,24 @@ def tile_attributeembeddinglayer_kernel(tc, table, src, v, b, att, offs, out):
     ):
         offsets = held.tile([P, NPIECES * OFFS_COLS], U16, name="offsets")
         nc.sync.dma_start(offsets[:], offs)
-        src_sb = held.tile([P, NB, H], BF16, name="src_sb")
-        nc.sync.dma_start(src_sb[:], src.rearrange("(n p) i -> p n i", p=P))
         b_col = held.tile([P, NB], F32, name="b_col")
         att_col = held.tile([P, NB], BF16, name="att_col")
         with nc.allow_non_contiguous_dma(reason="one element to a partition: 1024 small pieces, once"):
-            nc.gpsimd.dma_start(b_col[:], b.rearrange("(n p) o -> p (n o)", p=P))
-            nc.gpsimd.dma_start(att_col[:], att.rearrange("(n p) o -> p (n o)", p=P))
+            nc.scalar.dma_start(b_col[:], b.rearrange("(n p) o -> p (n o)", p=P))
+            nc.scalar.dma_start(att_col[:], att.rearrange("(n p) o -> p (n o)", p=P))
+        src_sb = held.tile([P, NB, H], BF16, name="src_sb")
+        nc.sync.dma_start(src_sb[:], src.rearrange("(n p) i -> p n i", p=P))
+        v_by_rows = v.rearrange("(n p) c -> p n c", p=P)
         v_sb = []
         table_sb = []
-        for n in range(NB):
-            v_rows = held.tile([P, C], BF16, name=f"v{n}")
-            nc.sync.dma_start(v_rows[:], v[n * P : (n + 1) * P, :])
-            v_sb.append(v_rows)
-            table_rows = held.tile([P, S], F32, name=f"table{n}")
-            nc.scalar.dma_start(table_rows[:], table[n * P : (n + 1) * P, :])
-            table_sb.append(table_rows)
+        for g in range(NB // V_BLOCKS):
+            v_group = held.tile([P, NB, V_BLOCKS * P], BF16, name=f"v{g}")
+            nc.sync.dma_start(v_group[:], v_by_rows[:, :, g * V_BLOCKS * P : (g + 1) * V_BLOCKS * P])
+            v_sb.append(v_group)
+            for cb in range(g * V_BLOCKS, (g + 1) * V_BLOCKS):
+                table_rows = held.tile([P, S], F32, name=f"table{cb}")
+                nc.scalar.dma_start(table_rows[:], table[cb * P : (cb + 1) * P, :])
+                table_sb.append(table_rows)
 
         ident_f32 = held.tile([P, P], F32, name="ident_f32")
         make_identity(nc, ident_f32[:])
@@ -59,7 +62,7 @@ def tile_attributeembeddinglayer_kernel(tc, table, src, v, b, att, offs, out):
         ones_bf = held.tile([P, P], BF16, name="ones_bf")
         nc.gpsimd.memset(ones_bf[:], 1.0)
         att_rep = held.tile([P, NB, P], BF16, name="att_rep")
-        nc.vector.tensor_copy(att_rep[:], att_col[:].unsqueeze(2).to_broadcast([P, NB, P]))
+        nc.gpsimd.tensor_copy(att_rep[:], att_col[:].unsqueeze(2).to_broadcast([P, NB, P]))
 
         u_sb = []
         for cb in range(NB):
@@ -67,7 +70,7 @@ def tile_attributeembeddinglayer_kernel(tc, table, src, v, b, att, offs, out):
             for eb in range(NB):
                 nc.tensor.matmul(
                     u_ps[:],
-                    lhsT=v_sb[eb][:, cb * P : (cb + 1) * P],
+                    lhsT=v_sb[cb // V_BLOCKS][:, eb, (cb % V_BLOCKS) * P : (cb % V_BLOCKS + 1) * P],
                     rhs=src_sb[:, eb, :],
                     start=(eb == 0),
                     stop=(eb == NB - 1),

@@ -15,7 +15,6 @@ PIECE_SLOTS = 2
 PIECE = PIECE_SLOTS * H
 NPIECES = K // PIECE_SLOTS
 OFFS_COLS = PIECE // 16
-V_BLOCKS = 2
 BANK = 512
 SLOTS_IN_BANK = BANK // H
 NBANKS = K // SLOTS_IN_BANK
@@ -44,14 +43,16 @@ def tile_attributeembeddinglayer_kernel(tc, table, src, v, b, att, offs, out):
         v_by_rows = v.rearrange("(n p) c -> p n c", p=P)
         v_sb = []
         table_sb = []
-        for g in range(NB // V_BLOCKS):
-            v_group = held.tile([P, NB, V_BLOCKS * P], BF16, name=f"v{g}")
-            nc.sync.dma_start(v_group[:], v_by_rows[:, :, g * V_BLOCKS * P : (g + 1) * V_BLOCKS * P])
-            v_sb.append(v_group)
-            for cb in range(g * V_BLOCKS, (g + 1) * V_BLOCKS):
-                table_rows = held.tile([P, S], F32, name=f"table{cb}")
-                nc.scalar.dma_start(table_rows[:], table[cb * P : (cb + 1) * P, :])
-                table_sb.append(table_rows)
+        for cb in range(NB):
+            v_block = held.tile([P, NB, P], BF16, name=f"v{cb}")
+            nc.sync.dma_start(v_block[:], v_by_rows[:, :, cb * P : (cb + 1) * P])
+            v_sb.append(v_block)
+            table_rows = held.tile([P, S], F32, name=f"table{cb}")
+            nc.scalar.dma_start(table_rows[:], table[cb * P : (cb + 1) * P, :])
+            table_sb.append(table_rows)
+        warm = held.tile([P, 1], F32, name="warm")
+        nc.gpsimd.memset(warm[:], 0.0)
+        nc.scalar.activation(warm[:], warm[:], ACT.Tanh)
 
         ident_f32 = held.tile([P, P], F32, name="ident_f32")
         make_identity(nc, ident_f32[:])
@@ -70,7 +71,7 @@ def tile_attributeembeddinglayer_kernel(tc, table, src, v, b, att, offs, out):
             for eb in range(NB):
                 nc.tensor.matmul(
                     u_ps[:],
-                    lhsT=v_sb[cb // V_BLOCKS][:, eb, (cb % V_BLOCKS) * P : (cb % V_BLOCKS + 1) * P],
+                    lhsT=v_sb[cb][:, eb, :],
                     rhs=src_sb[:, eb, :],
                     start=(eb == 0),
                     stop=(eb == NB - 1),

@@ -15,6 +15,7 @@ PIECE_SLOTS = 2
 PIECE = PIECE_SLOTS * H
 NPIECES = K // PIECE_SLOTS
 OFFS_COLS = PIECE // 16
+V_BLOCKS = 2
 BANK = 512
 SLOTS_IN_BANK = BANK // H
 NBANKS = K // SLOTS_IN_BANK
@@ -28,30 +29,39 @@ def tile_attributeembeddinglayer_kernel(tc, table, src, v, b, att, offs, out):
     with (
         tc.tile_pool(name="held", bufs=1) as held,
         tc.tile_pool(name="work", bufs=4) as work,
+        tc.tile_pool(name="sums", bufs=12) as sums,
         tc.psum_pool(name="block_psum", bufs=2) as block_psum,
         tc.psum_pool(name="logit_psum", bufs=1) as logit_psum,
     ):
+        v_by_rows = v.rearrange("(n p) c -> p n c", p=P)
+        v_sb = [held.tile([P, NB, V_BLOCKS * P], BF16, name=f"v{g}") for g in range(NB // V_BLOCKS)]
+        table_sb = [held.tile([P, S], F32, name=f"table{cb}") for cb in range(NB)]
         offsets = held.tile([P, NPIECES * OFFS_COLS], U16, name="offsets")
-        nc.sync.dma_start(offsets[:], offs)
+        src_sb = held.tile([P, NB, H], BF16, name="src_sb")
         b_col = held.tile([P, NB], F32, name="b_col")
         att_col = held.tile([P, NB], BF16, name="att_col")
+
+        def load_v(g):
+            nc.sync.dma_start(v_sb[g][:], v_by_rows[:, :, g * V_BLOCKS * P : (g + 1) * V_BLOCKS * P])
+
+        def load_table(queue, cb):
+            queue.dma_start(table_sb[cb][:], table[cb * P : (cb + 1) * P, :])
+
+        load_v(0)
+        nc.scalar.dma_start(src_sb[:], src.rearrange("(n p) i -> p n i", p=P))
+        nc.sync.dma_start(offsets[:], offs)
+        load_table(nc.scalar, 0)
         with nc.allow_non_contiguous_dma(reason="one element to a partition: 1024 small pieces, once"):
-            nc.scalar.dma_start(b_col[:], b.rearrange("(n p) o -> p (n o)", p=P))
-            nc.scalar.dma_start(att_col[:], att.rearrange("(n p) o -> p (n o)", p=P))
-        src_sb = held.tile([P, NB, H], BF16, name="src_sb")
-        nc.sync.dma_start(src_sb[:], src.rearrange("(n p) i -> p n i", p=P))
-        v_by_rows = v.rearrange("(n p) c -> p n c", p=P)
-        v_sb = []
-        table_sb = []
-        for cb in range(NB):
-            v_block = held.tile([P, NB, P], BF16, name=f"v{cb}")
-            nc.sync.dma_start(v_block[:], v_by_rows[:, :, cb * P : (cb + 1) * P])
-            v_sb.append(v_block)
-            table_rows = held.tile([P, S], F32, name=f"table{cb}")
-            nc.scalar.dma_start(table_rows[:], table[cb * P : (cb + 1) * P, :])
-            table_sb.append(table_rows)
+            nc.sync.dma_start(b_col[:], b.rearrange("(n p) o -> p (n o)", p=P))
+            nc.sync.dma_start(att_col[:], att.rearrange("(n p) o -> p (n o)", p=P))
+        load_v(1)
+        load_v(2)
+        load_table(nc.sync, 1)
+        load_v(3)
+        for cb in range(2, NB):
+            load_table(nc.sync, cb)
         warm = held.tile([P, 1], F32, name="warm")
-        nc.gpsimd.memset(warm[:], 0.0)
+        nc.vector.memset(warm[:], 0.0)
         nc.scalar.activation(warm[:], warm[:], ACT.Tanh)
 
         ident_f32 = held.tile([P, P], F32, name="ident_f32")
@@ -71,7 +81,7 @@ def tile_attributeembeddinglayer_kernel(tc, table, src, v, b, att, offs, out):
             for eb in range(NB):
                 nc.tensor.matmul(
                     u_ps[:],
-                    lhsT=v_sb[cb][:, eb, :],
+                    lhsT=v_sb[cb // V_BLOCKS][:, eb, (cb % V_BLOCKS) * P : (cb % V_BLOCKS + 1) * P],
                     rhs=src_sb[:, eb, :],
                     start=(eb == 0),
                     stop=(eb == NB - 1),
@@ -88,7 +98,7 @@ def tile_attributeembeddinglayer_kernel(tc, table, src, v, b, att, offs, out):
         for cb in range(NB):
             h = work.tile([P, K * H], BF16, name="h")
             for q in range(NPIECES):
-                z = work.tile([P, PIECE], F32, name="z")
+                z = sums.tile([P, PIECE], F32, name="z")
                 picked = table_sb[cb][:].indirect(offsets[:, q * OFFS_COLS : (q + 1) * OFFS_COLS])
                 nc.vector.tensor_tensor(z[:], picked, u_sb[cb][:], ALU.add)
                 nc.scalar.activation(h[:, q * PIECE : (q + 1) * PIECE], z[:], ACT.Tanh)
@@ -111,17 +121,18 @@ def tile_attributeembeddinglayer_kernel(tc, table, src, v, b, att, offs, out):
 
         neg_top = held.tile([P, 1], F32, name="neg_top")
         nc.vector.tensor_reduce(out=neg_top[:], in_=s_node[:], axis=AXIS_X, op=ALU.max, negate=True)
-        neg_shift_diag = held.tile([P, P], BF16, name="neg_shift_diag")
-        nc.vector.tensor_scalar(neg_shift_diag[:], ident_bf[:], neg_top[:, 0:1], 0.0, op0=ALU.mult, op1=ALU.min)
         neg_shift = held.tile([P, 1], BF16, name="neg_shift")
         nc.vector.tensor_scalar_min(neg_shift[:], neg_top[:], 0.0)
-        for j in range(NBANKS):
+        neg_shift_diag = held.tile([P, P], BF16, name="neg_shift_diag")
+        nc.vector.tensor_scalar(neg_shift_diag[:], ident_bf[:], neg_top[:, 0:1], 0.0, op0=ALU.mult, op1=ALU.min)
+        for q in range(NPIECES):
+            bank, in_bank = divmod(q * PIECE, BANK)
             nc.tensor.matmul(
-                s_bank[j][:].rearrange("p (k i) -> p k i", k=SLOTS_IN_BANK),
+                s_bank[bank][:, in_bank : in_bank + PIECE].rearrange("p (t i) -> p t i", t=PIECE_SLOTS),
                 lhsT=ones_bf[:],
-                rhs=neg_shift_diag[:].unsqueeze(1).to_broadcast([P, SLOTS_IN_BANK, H]),
+                rhs=neg_shift_diag[:].unsqueeze(1).to_broadcast([P, PIECE_SLOTS, H]),
                 start=False,
-                stop=True,
+                stop=(in_bank + PIECE == BANK),
             )
         e_node = held.tile([P, K], F32, name="e_node")
         e_node_sum = held.tile([P, 1], F32, name="e_node_sum")

@@ -1,3 +1,5 @@
+import math
+
 import concourse.mybir as mybir
 from concourse.masks import make_identity
 
@@ -16,9 +18,6 @@ PIECE = PIECE_SLOTS * H
 NPIECES = K // PIECE_SLOTS
 OFFS_COLS = PIECE // 16
 V_BLOCKS = 2
-BANK = 512
-SLOTS_IN_BANK = BANK // H
-NBANKS = K // SLOTS_IN_BANK
 UNLISTED = float(S - K)
 
 FLOPS = 2 * C * C * H + 2 * C * K * H
@@ -30,7 +29,7 @@ def tile_attributeembeddinglayer_kernel(tc, table, src, v, b, att, offs, out):
         tc.tile_pool(name="held", bufs=1) as held,
         tc.tile_pool(name="work", bufs=4) as work,
         tc.tile_pool(name="sums", bufs=12) as sums,
-        tc.psum_pool(name="block_psum", bufs=2) as block_psum,
+        tc.psum_pool(name="block_psum", bufs=3) as block_psum,
         tc.psum_pool(name="logit_psum", bufs=1) as logit_psum,
     ):
         v_by_rows = v.rearrange("(n p) c -> p n c", p=P)
@@ -68,16 +67,12 @@ def tile_attributeembeddinglayer_kernel(tc, table, src, v, b, att, offs, out):
         make_identity(nc, ident_f32[:])
         ident_bf = held.tile([P, P], BF16, name="ident_bf")
         make_identity(nc, ident_bf[:])
-        ones_f32 = held.tile([P, P], F32, name="ones_f32")
-        nc.gpsimd.memset(ones_f32[:], 1.0)
-        ones_bf = held.tile([P, P], BF16, name="ones_bf")
-        nc.gpsimd.memset(ones_bf[:], 1.0)
-        att_rep = held.tile([P, NB, P], BF16, name="att_rep")
-        nc.gpsimd.tensor_copy(att_rep[:], att_col[:].unsqueeze(2).to_broadcast([P, NB, P]))
+        ln_unlisted = held.tile([P, 1], F32, name="ln_unlisted")
+        nc.gpsimd.memset(ln_unlisted[:], math.log(UNLISTED))
 
         u_sb = []
         for cb in range(NB):
-            u_ps = block_psum.tile([P, H], F32, name="u_ps")
+            u_ps = block_psum.tile([P, H], F32, name="u_ps", tag="block")
             for eb in range(NB):
                 nc.tensor.matmul(
                     u_ps[:],
@@ -93,8 +88,8 @@ def tile_attributeembeddinglayer_kernel(tc, table, src, v, b, att, offs, out):
                 )
             u_sb.append(u_block)
 
-        s_bank = [logit_psum.tile([P, BANK], F32, name=f"s_bank{j}") for j in range(NBANKS)]
-        s_node = logit_psum.tile([P, K], F32, name="s_node")
+        s_node = logit_psum.tile([P, K + 1], F32, name="s_node")
+        nc.tensor.matmul(s_node[:, K : K + 1], lhsT=ident_f32[:], rhs=ln_unlisted[:], start=True, stop=False)
         for cb in range(NB):
             h = work.tile([P, K * H], BF16, name="h")
             for q in range(NPIECES):
@@ -107,65 +102,33 @@ def tile_attributeembeddinglayer_kernel(tc, table, src, v, b, att, offs, out):
                         s_node[:, k : k + 1],
                         lhsT=h[:, k * H : (k + 1) * H],
                         rhs=att_col[:, cb : cb + 1],
-                        start=(cb == 0 and k == 0),
+                        start=False,
                         stop=(cb == NB - 1 and k == K - 1),
                     )
-                bank, in_bank = divmod(q * PIECE, BANK)
-                nc.tensor.matmul(
-                    s_bank[bank][:, in_bank : in_bank + PIECE],
-                    lhsT=att_rep[:, cb, :],
-                    rhs=h[:, q * PIECE : (q + 1) * PIECE],
-                    start=(cb == 0 and in_bank == 0),
-                    stop=False,
-                )
 
-        neg_top = held.tile([P, 1], F32, name="neg_top")
-        nc.vector.tensor_reduce(out=neg_top[:], in_=s_node[:], axis=AXIS_X, op=ALU.max, negate=True)
-        neg_shift = held.tile([P, 1], BF16, name="neg_shift")
-        nc.vector.tensor_scalar_min(neg_shift[:], neg_top[:], 0.0)
-        neg_shift_diag = held.tile([P, P], BF16, name="neg_shift_diag")
-        nc.vector.tensor_scalar(neg_shift_diag[:], ident_bf[:], neg_top[:, 0:1], 0.0, op0=ALU.mult, op1=ALU.min)
-        for q in range(NPIECES):
-            bank, in_bank = divmod(q * PIECE, BANK)
-            nc.tensor.matmul(
-                s_bank[bank][:, in_bank : in_bank + PIECE].rearrange("p (t i) -> p t i", t=PIECE_SLOTS),
-                lhsT=ones_bf[:],
-                rhs=neg_shift_diag[:].unsqueeze(1).to_broadcast([P, PIECE_SLOTS, H]),
-                start=False,
-                stop=(in_bank + PIECE == BANK),
-            )
-        e_node = held.tile([P, K], F32, name="e_node")
-        e_node_sum = held.tile([P, 1], F32, name="e_node_sum")
-        nc.scalar.activation(e_node[:], s_node[:], ACT.Exp, bias=neg_shift[:, 0:1], accum_out=e_node_sum[:])
-        e_zero = held.tile([P, 1], F32, name="e_zero")
-        nc.scalar.activation(e_zero[:], neg_shift[:], ACT.Exp)
+        neg_shift = held.tile([P, 1], F32, name="neg_shift")
+        nc.vector.tensor_reduce(out=neg_shift[:], in_=s_node[:], axis=AXIS_X, op=ALU.max, negate=True)
+        e_node = held.tile([P, K + 1], F32, name="e_node")
         denom = held.tile([P, 1], F32, name="denom")
-        nc.vector.scalar_tensor_tensor(denom[:], e_zero[:], UNLISTED, e_node_sum[:], op0=ALU.mult, op1=ALU.add)
+        nc.scalar.activation(e_node[:], s_node[:], ACT.Exp, bias=neg_shift[:, 0:1], accum_out=denom[:])
         recip = held.tile([P, 1], F32, name="recip")
         nc.vector.reciprocal(recip[:], denom[:])
-        recip_diag = held.tile([P, P], F32, name="recip_diag")
-        nc.vector.tensor_scalar_mul(recip_diag[:], ident_f32[:], recip[:, 0:1])
-        recip_rep = logit_psum.tile([P, H], F32, name="recip_rep")
-        nc.tensor.matmul(recip_rep[:], lhsT=ones_f32[:], rhs=recip_diag[:], start=True, stop=True)
-        e = held.tile([P, K * H], F32, name="e")
+        a_node = held.tile([P, K], F32, name="a_node")
+        nc.vector.tensor_scalar_mul(a_node[:], e_node[:, 0:K], recip[:, 0:1])
         a = held.tile([P, K * H], F32, name="a")
         for q in range(NPIECES):
-            bank, in_bank = divmod(q * PIECE, BANK)
-            nc.scalar.activation(
-                e[:, q * PIECE : (q + 1) * PIECE], s_bank[bank][:, in_bank : in_bank + PIECE], ACT.Exp
-            )
+            a_ps = logit_psum.tile([P, PIECE], F32, name=f"a_ps{q}")
+            for t in range(PIECE_SLOTS):
+                k = q * PIECE_SLOTS + t
+                nc.tensor.transpose(
+                    a_ps[:, t * H : (t + 1) * H], a_node[:, k : k + 1].to_broadcast([P, P]), ident_f32[:]
+                )
+            nc.scalar.copy(a[:, q * PIECE : (q + 1) * PIECE], a_ps[:])
 
         for cb in range(NB):
-            acc = block_psum.tile([P, H], F32, name="acc")
+            acc = block_psum.tile([P, H], F32, name="acc", tag="block")
             nc.tensor.matmul(acc[:], lhsT=ident_bf[:], rhs=src_sb[:, cb, :], start=True, stop=False)
             for q in range(NPIECES):
-                if cb == 0:
-                    nc.vector.tensor_tensor(
-                        a[:, q * PIECE : (q + 1) * PIECE].rearrange("p (t i) -> p t i", t=PIECE_SLOTS),
-                        e[:, q * PIECE : (q + 1) * PIECE].rearrange("p (t i) -> p t i", t=PIECE_SLOTS),
-                        recip_rep[:].unsqueeze(1).to_broadcast([P, PIECE_SLOTS, H]),
-                        ALU.mult,
-                    )
                 prod = work.tile([P, PIECE], F32, name="prod")
                 picked = table_sb[cb][:].indirect(offsets[:, q * OFFS_COLS : (q + 1) * OFFS_COLS])
                 nc.vector.tensor_tensor(prod[:], picked, a[:, q * PIECE : (q + 1) * PIECE], ALU.mult)

@@ -15,8 +15,10 @@ C, S, K, H = 1024, 256, 8, 128
 NB = C // P
 PIECE_SLOTS = 2
 PIECE = PIECE_SLOTS * H
-NPIECES = K // PIECE_SLOTS
-OFFS_COLS = PIECE // 16
+SLOT_COLS = H // 16
+PAIRS = [(k, k + PIECE_SLOTS) for k in range(0, K, PIECE_SLOTS)]
+LAST_PAIR_CUT = PAIRS[:-1] + [(K - 2, K - 1), (K - 1, K)]
+FIRST_PAIR_CUT = [(0, 1), (1, 2)] + PAIRS[1:]
 V_BLOCKS = 2
 UNLISTED = float(S - K)
 
@@ -29,13 +31,14 @@ def tile_attributeembeddinglayer_kernel(tc, table, src, v, b, att, offs, out):
         tc.tile_pool(name="held", bufs=1) as held,
         tc.tile_pool(name="work", bufs=4) as work,
         tc.tile_pool(name="sums", bufs=12) as sums,
-        tc.psum_pool(name="block_psum", bufs=3) as block_psum,
+        tc.psum_pool(name="block_psum", bufs=2) as block_psum,
         tc.psum_pool(name="logit_psum", bufs=1) as logit_psum,
     ):
-        v_by_rows = v.rearrange("(n p) c -> p n c", p=P)
+        v_by_rows = v.rearrange("(p n) c -> p n c", n=NB)
         v_sb = [held.tile([P, NB, V_BLOCKS * P], BF16, name=f"v{g}") for g in range(NB // V_BLOCKS)]
         table_sb = [held.tile([P, S], F32, name=f"table{cb}") for cb in range(NB)]
-        offsets = held.tile([P, NPIECES * OFFS_COLS], U16, name="offsets")
+        offsets = held.tile([P, K * SLOT_COLS], U16, name="offsets")
+        src_for_u = held.tile([P, NB, H], BF16, name="src_for_u")
         src_sb = held.tile([P, NB, H], BF16, name="src_sb")
         b_col = held.tile([P, NB], F32, name="b_col")
         att_col = held.tile([P, NB], BF16, name="att_col")
@@ -47,7 +50,7 @@ def tile_attributeembeddinglayer_kernel(tc, table, src, v, b, att, offs, out):
             queue.dma_start(table_sb[cb][:], table[cb * P : (cb + 1) * P, :])
 
         load_v(0)
-        nc.scalar.dma_start(src_sb[:], src.rearrange("(n p) i -> p n i", p=P))
+        nc.scalar.dma_start(src_for_u[:], src.rearrange("(p n) i -> p n i", n=NB))
         nc.sync.dma_start(offsets[:], offs)
         load_table(nc.scalar, 0)
         with nc.allow_non_contiguous_dma(reason="one element to a partition: 1024 small pieces, once"):
@@ -59,6 +62,7 @@ def tile_attributeembeddinglayer_kernel(tc, table, src, v, b, att, offs, out):
         load_v(3)
         for cb in range(2, NB):
             load_table(nc.sync, cb)
+        nc.sync.dma_start(src_sb[:], src.rearrange("(n p) i -> p n i", p=P))
         warm = held.tile([P, 1], F32, name="warm")
         nc.vector.memset(warm[:], 0.0)
         nc.scalar.activation(warm[:], warm[:], ACT.Tanh)
@@ -77,27 +81,30 @@ def tile_attributeembeddinglayer_kernel(tc, table, src, v, b, att, offs, out):
                 nc.tensor.matmul(
                     u_ps[:],
                     lhsT=v_sb[cb // V_BLOCKS][:, eb, (cb % V_BLOCKS) * P : (cb % V_BLOCKS + 1) * P],
-                    rhs=src_sb[:, eb, :],
+                    rhs=src_for_u[:, eb, :],
                     start=(eb == 0),
                     stop=(eb == NB - 1),
                 )
             u_block = held.tile([P, PIECE], F32, name=f"u{cb}")
-            for t in range(PIECE_SLOTS):
-                nc.scalar.activation(
-                    u_block[:, t * H : (t + 1) * H], u_ps[:], ACT.Identity, bias=b_col[:, cb : cb + 1]
-                )
+            nc.scalar.activation(
+                u_block[:].rearrange("p (t i) -> p t i", t=PIECE_SLOTS),
+                u_ps[:].unsqueeze(1).to_broadcast([P, PIECE_SLOTS, H]),
+                ACT.Identity,
+                bias=b_col[:, cb : cb + 1],
+            )
             u_sb.append(u_block)
 
         s_node = logit_psum.tile([P, K + 1], F32, name="s_node")
         nc.tensor.matmul(s_node[:, K : K + 1], lhsT=ident_f32[:], rhs=ln_unlisted[:], start=True, stop=False)
         for cb in range(NB):
             h = work.tile([P, K * H], BF16, name="h")
-            for q in range(NPIECES):
+            for k0, k1 in LAST_PAIR_CUT if cb == NB - 1 else PAIRS:
+                width = (k1 - k0) * H
                 z = sums.tile([P, PIECE], F32, name="z")
-                picked = table_sb[cb][:].indirect(offsets[:, q * OFFS_COLS : (q + 1) * OFFS_COLS])
-                nc.vector.tensor_tensor(z[:], picked, u_sb[cb][:], ALU.add)
-                nc.scalar.activation(h[:, q * PIECE : (q + 1) * PIECE], z[:], ACT.Tanh)
-                for k in range(q * PIECE_SLOTS, (q + 1) * PIECE_SLOTS):
+                picked = table_sb[cb][:].indirect(offsets[:, k0 * SLOT_COLS : k1 * SLOT_COLS])
+                nc.vector.tensor_tensor(z[:, 0:width], picked, u_sb[cb][:, 0:width], ALU.add)
+                nc.scalar.activation(h[:, k0 * H : k1 * H], z[:, 0:width], ACT.Tanh)
+                for k in range(k0, k1):
                     nc.tensor.matmul(
                         s_node[:, k : k + 1],
                         lhsT=h[:, k * H : (k + 1) * H],
@@ -116,29 +123,28 @@ def tile_attributeembeddinglayer_kernel(tc, table, src, v, b, att, offs, out):
         a_node = held.tile([P, K], F32, name="a_node")
         nc.vector.tensor_scalar_mul(a_node[:], e_node[:, 0:K], recip[:, 0:1])
         a = held.tile([P, K * H], F32, name="a")
-        for q in range(NPIECES):
-            a_ps = logit_psum.tile([P, PIECE], F32, name=f"a_ps{q}")
-            for t in range(PIECE_SLOTS):
-                k = q * PIECE_SLOTS + t
+        for k0, k1 in FIRST_PAIR_CUT:
+            a_ps = logit_psum.tile([P, (k1 - k0) * H], F32, name=f"a_ps{k0}")
+            for k in range(k0, k1):
                 nc.tensor.transpose(
-                    a_ps[:, t * H : (t + 1) * H], a_node[:, k : k + 1].to_broadcast([P, P]), ident_f32[:]
+                    a_ps[:, (k - k0) * H : (k - k0 + 1) * H], a_node[:, k : k + 1].to_broadcast([P, P]), ident_f32[:]
                 )
-            nc.scalar.copy(a[:, q * PIECE : (q + 1) * PIECE], a_ps[:])
+            nc.scalar.copy(a[:, k0 * H : k1 * H], a_ps[:])
 
         for cb in range(NB):
             acc = block_psum.tile([P, H], F32, name="acc", tag="block")
             nc.tensor.matmul(acc[:], lhsT=ident_bf[:], rhs=src_sb[:, cb, :], start=True, stop=False)
-            for q in range(NPIECES):
+            for k0, k1 in FIRST_PAIR_CUT if cb == 0 else PAIRS:
                 prod = work.tile([P, PIECE], F32, name="prod")
-                picked = table_sb[cb][:].indirect(offsets[:, q * OFFS_COLS : (q + 1) * OFFS_COLS])
-                nc.vector.tensor_tensor(prod[:], picked, a[:, q * PIECE : (q + 1) * PIECE], ALU.mult)
-                for t in range(PIECE_SLOTS):
+                picked = table_sb[cb][:].indirect(offsets[:, k0 * SLOT_COLS : k1 * SLOT_COLS])
+                nc.vector.tensor_tensor(prod[:, 0 : (k1 - k0) * H], picked, a[:, k0 * H : k1 * H], ALU.mult)
+                for k in range(k0, k1):
                     nc.tensor.matmul(
                         acc[:],
                         lhsT=ident_f32[:],
-                        rhs=prod[:, t * H : (t + 1) * H],
+                        rhs=prod[:, (k - k0) * H : (k - k0 + 1) * H],
                         start=False,
-                        stop=(q == NPIECES - 1 and t == PIECE_SLOTS - 1),
+                        stop=(k == K - 1),
                     )
             res = work.tile([P, H], F32, name="res")
             nc.scalar.copy(res[:], acc[:])

@@ -43,25 +43,23 @@ def tile_attributeembeddinglayer_kernel(tc, table, src, v, b, att, offs, out):
         b_col = held.tile([P, NB], F32, name="b_col")
         att_col = held.tile([P, NB], BF16, name="att_col")
 
-        def load_v(g):
-            nc.sync.dma_start(v_sb[g][:], v_by_rows[:, :, g * V_BLOCKS * P : (g + 1) * V_BLOCKS * P])
-
         def load_table(queue, cb):
             queue.dma_start(table_sb[cb][:], table[cb * P : (cb + 1) * P, :])
 
-        load_v(0)
         nc.scalar.dma_start(src_for_u[:], src.rearrange("(p n) i -> p n i", n=NB))
-        nc.sync.dma_start(offsets[:], offs)
+        with nc.allow_non_contiguous_dma(reason="one element to a partition: 1024 small pieces, once"):
+            nc.scalar.dma_start(b_col[:], b.rearrange("(n p) o -> p (n o)", p=P))
         load_table(nc.scalar, 0)
         with nc.allow_non_contiguous_dma(reason="one element to a partition: 1024 small pieces, once"):
-            nc.sync.dma_start(b_col[:], b.rearrange("(n p) o -> p (n o)", p=P))
-            nc.sync.dma_start(att_col[:], att.rearrange("(n p) o -> p (n o)", p=P))
-        load_v(1)
-        load_v(2)
-        load_table(nc.sync, 1)
-        load_v(3)
-        for cb in range(2, NB):
-            load_table(nc.sync, cb)
+            nc.scalar.dma_start(att_col[:], att.rearrange("(n p) o -> p (n o)", p=P))
+        for cb in range(NB):
+            if cb % V_BLOCKS == 0:
+                g = cb // V_BLOCKS
+                nc.sync.dma_start(v_sb[g][:], v_by_rows[:, :, g * V_BLOCKS * P : (g + 1) * V_BLOCKS * P])
+            if cb == 0:
+                nc.sync.dma_start(offsets[:], offs)
+            else:
+                load_table(nc.sync, cb)
         nc.sync.dma_start(src_sb[:], src.rearrange("(n p) i -> p n i", p=P))
         warm = held.tile([P, 1], F32, name="warm")
         nc.vector.memset(warm[:], 0.0)

@@ -40,26 +40,19 @@ def tile_attributeembeddinglayer_kernel(tc, table, src, v, b, att, offs, out):
         offsets = held.tile([P, K * SLOT_COLS], U16, name="offsets")
         src_for_u = held.tile([P, NB, H], BF16, name="src_for_u")
         src_sb = held.tile([P, NB, H], BF16, name="src_sb")
-        b_col = held.tile([P, NB], F32, name="b_col")
-        att_col = held.tile([P, NB], BF16, name="att_col")
-
-        def load_table(queue, cb):
-            queue.dma_start(table_sb[cb][:], table[cb * P : (cb + 1) * P, :])
+        b_rows = held.tile([NB, P], F32, name="b_rows")
+        att_rows = held.tile([NB, P], BF16, name="att_rows")
+        nc.sync.dma_start(b_rows[:], b.rearrange("(n p) o -> n (p o)", p=P))
+        nc.sync.dma_start(att_rows[:], att.rearrange("(n p) o -> n (p o)", p=P))
 
         nc.scalar.dma_start(src_for_u[:], src.rearrange("(p n) i -> p n i", n=NB))
-        with nc.allow_non_contiguous_dma(reason="one element to a partition: 1024 small pieces, once"):
-            nc.scalar.dma_start(b_col[:], b.rearrange("(n p) o -> p (n o)", p=P))
-        load_table(nc.scalar, 0)
-        with nc.allow_non_contiguous_dma(reason="one element to a partition: 1024 small pieces, once"):
-            nc.scalar.dma_start(att_col[:], att.rearrange("(n p) o -> p (n o)", p=P))
         for cb in range(NB):
             if cb % V_BLOCKS == 0:
                 g = cb // V_BLOCKS
                 nc.sync.dma_start(v_sb[g][:], v_by_rows[:, :, g * V_BLOCKS * P : (g + 1) * V_BLOCKS * P])
             if cb == 0:
                 nc.sync.dma_start(offsets[:], offs)
-            else:
-                load_table(nc.sync, cb)
+            nc.sync.dma_start(table_sb[cb][:], table[cb * P : (cb + 1) * P, :])
         nc.sync.dma_start(src_sb[:], src.rearrange("(n p) i -> p n i", p=P))
         warm = held.tile([P, 1], F32, name="warm")
         nc.vector.memset(warm[:], 0.0)
@@ -72,23 +65,33 @@ def tile_attributeembeddinglayer_kernel(tc, table, src, v, b, att, offs, out):
         ln_unlisted = held.tile([P, 1], F32, name="ln_unlisted")
         nc.gpsimd.memset(ln_unlisted[:], math.log(UNLISTED))
 
+        att_ps = block_psum.tile([P, NB], F32, name="att_ps", tag="block")
+        nc.tensor.matmul(att_ps[:], lhsT=att_rows[:], rhs=ident_bf[0:NB, 0:NB], start=True, stop=True)
+        att_col = held.tile([P, NB], BF16, name="att_col")
+        nc.scalar.copy(att_col[:], att_ps[:])
+
         u_sb = []
         for cb in range(NB):
             u_ps = block_psum.tile([P, H], F32, name="u_ps", tag="block")
+            nc.tensor.matmul(
+                u_ps[:],
+                lhsT=b_rows[:],
+                rhs=ident_f32[0:NB, cb : cb + 1].to_broadcast([NB, H]),
+                start=True,
+                stop=False,
+            )
             for eb in range(NB):
                 nc.tensor.matmul(
                     u_ps[:],
                     lhsT=v_sb[cb // V_BLOCKS][:, eb, (cb % V_BLOCKS) * P : (cb % V_BLOCKS + 1) * P],
                     rhs=src_for_u[:, eb, :],
-                    start=(eb == 0),
+                    start=False,
                     stop=(eb == NB - 1),
                 )
             u_block = held.tile([P, PIECE], F32, name=f"u{cb}")
-            nc.scalar.activation(
+            nc.scalar.copy(
                 u_block[:].rearrange("p (t i) -> p t i", t=PIECE_SLOTS),
                 u_ps[:].unsqueeze(1).to_broadcast([P, PIECE_SLOTS, H]),
-                ACT.Identity,
-                bias=b_col[:, cb : cb + 1],
             )
             u_sb.append(u_block)
 

@@ -20,6 +20,7 @@ PAIRS = [(k, k + PIECE_SLOTS) for k in range(0, K, PIECE_SLOTS)]
 LAST_PAIR_CUT = PAIRS[:-1] + [(K - 2, K - 1), (K - 1, K)]
 FIRST_PAIR_CUT = [(0, 1), (1, 2)] + PAIRS[1:]
 V_BLOCKS = 2
+V_PARTS = 2
 UNLISTED = float(S - K)
 
 FLOPS = 2 * C * C * H + 2 * C * K * H
@@ -35,7 +36,10 @@ def tile_attributeembeddinglayer_kernel(tc, table, src, v, b, att, offs, out):
         tc.psum_pool(name="logit_psum", bufs=1) as logit_psum,
     ):
         v_by_rows = v.rearrange("(p n) c -> p n c", n=NB)
-        v_sb = [held.tile([P, NB, V_BLOCKS * P], BF16, name=f"v{g}") for g in range(NB // V_BLOCKS)]
+        v_sb = [
+            [held.tile([P, NB // V_PARTS, V_BLOCKS * P], BF16, name=f"v{g}_{part}") for part in range(V_PARTS)]
+            for g in range(NB // V_BLOCKS)
+        ]
         table_sb = [held.tile([P, S], F32, name=f"table{cb}") for cb in range(NB)]
         offsets = held.tile([P, K * SLOT_COLS], U16, name="offsets")
         src_for_u = held.tile([P, NB, H], BF16, name="src_for_u")
@@ -49,7 +53,15 @@ def tile_attributeembeddinglayer_kernel(tc, table, src, v, b, att, offs, out):
         for cb in range(NB):
             if cb % V_BLOCKS == 0:
                 g = cb // V_BLOCKS
-                nc.sync.dma_start(v_sb[g][:], v_by_rows[:, :, g * V_BLOCKS * P : (g + 1) * V_BLOCKS * P])
+                for part in range(V_PARTS):
+                    nc.sync.dma_start(
+                        v_sb[g][part][:],
+                        v_by_rows[
+                            :,
+                            part * (NB // V_PARTS) : (part + 1) * (NB // V_PARTS),
+                            g * V_BLOCKS * P : (g + 1) * V_BLOCKS * P,
+                        ],
+                    )
             if cb == 0:
                 nc.sync.dma_start(offsets[:], offs)
             nc.sync.dma_start(table_sb[cb][:], table[cb * P : (cb + 1) * P, :])
@@ -83,7 +95,9 @@ def tile_attributeembeddinglayer_kernel(tc, table, src, v, b, att, offs, out):
             for eb in range(NB):
                 nc.tensor.matmul(
                     u_ps[:],
-                    lhsT=v_sb[cb // V_BLOCKS][:, eb, (cb % V_BLOCKS) * P : (cb % V_BLOCKS + 1) * P],
+                    lhsT=v_sb[cb // V_BLOCKS][eb // (NB // V_PARTS)][
+                        :, eb % (NB // V_PARTS), (cb % V_BLOCKS) * P : (cb % V_BLOCKS + 1) * P
+                    ],
                     rhs=src_for_u[:, eb, :],
                     start=False,
                     stop=(eb == NB - 1),

@@ -20,7 +20,7 @@ PAIRS = [(k, k + PIECE_SLOTS) for k in range(0, K, PIECE_SLOTS)]
 LAST_PAIR_CUT = PAIRS[:-1] + [(K - 2, K - 1), (K - 1, K)]
 FIRST_PAIR_CUT = [(0, 1), (1, 2)] + PAIRS[1:]
 V_BLOCKS = 2
-V_PARTS = 2
+V_PARTS = 4
 UNLISTED = float(S - K)
 
 FLOPS = 2 * C * C * H + 2 * C * K * H

@@ -42,14 +42,18 @@ def tile_attributeembeddinglayer_kernel(tc, table, src, v, b, att, offs, out):
         ]
         table_sb = [held.tile([P, S], F32, name=f"table{cb}") for cb in range(NB)]
         offsets = held.tile([P, K * SLOT_COLS], U16, name="offsets")
-        src_for_u = held.tile([P, NB, H], BF16, name="src_for_u")
+        src_for_u = [held.tile([P, NB // V_PARTS, H], BF16, name=f"src_for_u{part}") for part in range(V_PARTS)]
         src_sb = held.tile([P, NB, H], BF16, name="src_sb")
         b_rows = held.tile([NB, P], F32, name="b_rows")
         att_rows = held.tile([NB, P], BF16, name="att_rows")
         nc.sync.dma_start(b_rows[:], b.rearrange("(n p) o -> n (p o)", p=P))
         nc.sync.dma_start(att_rows[:], att.rearrange("(n p) o -> n (p o)", p=P))
 
-        nc.scalar.dma_start(src_for_u[:], src.rearrange("(p n) i -> p n i", n=NB))
+        src_by_rows = src.rearrange("(p n) i -> p n i", n=NB)
+        for part in range(V_PARTS):
+            nc.scalar.dma_start(
+                src_for_u[part][:], src_by_rows[:, part * (NB // V_PARTS) : (part + 1) * (NB // V_PARTS), :]
+            )
         for cb in range(NB):
             if cb % V_BLOCKS == 0:
                 g = cb // V_BLOCKS
@@ -98,7 +102,7 @@ def tile_attributeembeddinglayer_kernel(tc, table, src, v, b, att, offs, out):
                     lhsT=v_sb[cb // V_BLOCKS][eb // (NB // V_PARTS)][
                         :, eb % (NB // V_PARTS), (cb % V_BLOCKS) * P : (cb % V_BLOCKS + 1) * P
                     ],
-                    rhs=src_for_u[:, eb, :],
+                    rhs=src_for_u[eb // (NB // V_PARTS)][:, eb % (NB // V_PARTS), :],
                     start=False,
                     stop=(eb == NB - 1),
                 )

@@ -151,20 +151,26 @@ def tile_attributeembeddinglayer_kernel(tc, table, src, v, b, att, offs, out):
             nc.scalar.copy(a[:, k0 * H : k1 * H], a_ps[:])
 
         for cb in range(NB):
+            on_tensor = K - PIECE_SLOTS if cb == NB - 1 else K
             acc = block_psum.tile([P, H], F32, name="acc", tag="block")
             nc.tensor.matmul(acc[:], lhsT=ident_bf[:], rhs=src_sb[:, cb, :], start=True, stop=False)
             for k0, k1 in FIRST_PAIR_CUT if cb == 0 else PAIRS:
                 prod = work.tile([P, PIECE], F32, name="prod")
                 picked = table_sb[cb][:].indirect(offsets[:, k0 * SLOT_COLS : k1 * SLOT_COLS])
                 nc.vector.tensor_tensor(prod[:, 0 : (k1 - k0) * H], picked, a[:, k0 * H : k1 * H], ALU.mult)
-                for k in range(k0, k1):
+                for k in range(k0, min(k1, on_tensor)):
                     nc.tensor.matmul(
                         acc[:],
                         lhsT=ident_f32[:],
                         rhs=prod[:, (k - k0) * H : (k - k0 + 1) * H],
                         start=False,
-                        stop=(k == K - 1),
+                        stop=(k == on_tensor - 1),
                     )
             res = work.tile([P, H], F32, name="res")
-            nc.scalar.copy(res[:], acc[:])
+            if cb == NB - 1:
+                pair_sum = work.tile([P, H], F32, name="pair_sum")
+                nc.vector.tensor_tensor(pair_sum[:], prod[:, 0:H], prod[:, H : 2 * H], ALU.add)
+                nc.vector.tensor_tensor(res[:], acc[:], pair_sum[:], ALU.add)
+            else:
+                nc.scalar.copy(res[:], acc[:])
             nc.sync.dma_start(out[cb * P : (cb + 1) * P, :], res[:])

@@ -107,10 +107,12 @@ def tile_attributeembeddinglayer_kernel(tc, table, src, v, b, att, offs, out):
                     stop=(eb == NB - 1),
                 )
             u_block = held.tile([P, PIECE], F32, name=f"u{cb}")
-            nc.scalar.copy(
-                u_block[:].rearrange("p (t i) -> p t i", t=PIECE_SLOTS),
-                u_ps[:].unsqueeze(1).to_broadcast([P, PIECE_SLOTS, H]),
-            )
+            u_copies = u_block[:].rearrange("p (t i) -> p t i", t=PIECE_SLOTS)
+            u_repeated = u_ps[:].unsqueeze(1).to_broadcast([P, PIECE_SLOTS, H])
+            if cb == 0:
+                nc.vector.tensor_copy(u_copies, u_repeated)
+            else:
+                nc.scalar.copy(u_copies, u_repeated)
             u_sb.append(u_block)
 
         s_node = logit_psum.tile([P, K + 1], F32, name="s_node")
@@ -148,7 +150,10 @@ def tile_attributeembeddinglayer_kernel(tc, table, src, v, b, att, offs, out):
                 nc.tensor.transpose(
                     a_ps[:, (k - k0) * H : (k - k0 + 1) * H], a_node[:, k : k + 1].to_broadcast([P, P]), ident_f32[:]
                 )
-            nc.scalar.copy(a[:, k0 * H : k1 * H], a_ps[:])
+            if k0 == 0:
+                nc.vector.tensor_copy(a[:, k0 * H : k1 * H], a_ps[:])
+            else:
+                nc.scalar.copy(a[:, k0 * H : k1 * H], a_ps[:])
 
         for cb in range(NB):
             on_tensor = K - PIECE_SLOTS if cb == NB - 1 else K

@@ -20,7 +20,7 @@ PAIRS = [(k, k + PIECE_SLOTS) for k in range(0, K, PIECE_SLOTS)]
 LAST_PAIR_CUT = PAIRS[:-1] + [(K - 2, K - 1), (K - 1, K)]
 FIRST_PAIR_CUT = [(0, 1), (1, 2)] + PAIRS[1:]
 V_BLOCKS = 2
-V_PARTS = 4
+V_PARTS = 2
 UNLISTED = float(S - K)
 
 FLOPS = 2 * C * C * H + 2 * C * K * H
@@ -81,21 +81,17 @@ def tile_attributeembeddinglayer_kernel(tc, table, src, v, b, att, offs, out):
         ln_unlisted = held.tile([P, 1], F32, name="ln_unlisted")
         nc.gpsimd.memset(ln_unlisted[:], math.log(UNLISTED))
 
-        att_ps = block_psum.tile([P, NB], F32, name="att_ps", tag="block")
-        nc.tensor.matmul(att_ps[:], lhsT=att_rows[:], rhs=ident_bf[0:NB, 0:NB], start=True, stop=True)
+        columns_ps = block_psum.tile([P, 2 * NB], F32, name="columns_ps", tag="block")
+        nc.tensor.matmul(columns_ps[:, 0:NB], lhsT=b_rows[:], rhs=ident_f32[0:NB, 0:NB], start=True, stop=True)
+        nc.tensor.matmul(columns_ps[:, NB : 2 * NB], lhsT=att_rows[:], rhs=ident_bf[0:NB, 0:NB], start=True, stop=True)
+        b_col = held.tile([P, NB], F32, name="b_col")
+        nc.vector.tensor_copy(b_col[:], columns_ps[:, 0:NB])
         att_col = held.tile([P, NB], BF16, name="att_col")
-        nc.scalar.copy(att_col[:], att_ps[:])
+        nc.vector.tensor_copy(att_col[:], columns_ps[:, NB : 2 * NB])
 
         u_sb = []
         for cb in range(NB):
             u_ps = block_psum.tile([P, H], F32, name="u_ps", tag="block")
-            nc.tensor.matmul(
-                u_ps[:],
-                lhsT=b_rows[:],
-                rhs=ident_f32[0:NB, cb : cb + 1].to_broadcast([NB, H]),
-                start=True,
-                stop=False,
-            )
             for eb in range(NB):
                 nc.tensor.matmul(
                     u_ps[:],
@@ -103,16 +99,16 @@ def tile_attributeembeddinglayer_kernel(tc, table, src, v, b, att, offs, out):
                         :, eb % (NB // V_PARTS), (cb % V_BLOCKS) * P : (cb % V_BLOCKS + 1) * P
                     ],
                     rhs=src_for_u[eb // (NB // V_PARTS)][:, eb % (NB // V_PARTS), :],
-                    start=False,
+                    start=(eb == 0),
                     stop=(eb == NB - 1),
                 )
             u_block = held.tile([P, PIECE], F32, name=f"u{cb}")
             u_copies = u_block[:].rearrange("p (t i) -> p t i", t=PIECE_SLOTS)
             u_repeated = u_ps[:].unsqueeze(1).to_broadcast([P, PIECE_SLOTS, H])
             if cb == 0:
-                nc.vector.tensor_copy(u_copies, u_repeated)
+                nc.vector.tensor_scalar_add(u_copies, u_repeated, b_col[:, cb : cb + 1])
             else:
-                nc.scalar.copy(u_copies, u_repeated)
+                nc.scalar.activation(u_copies, u_repeated, ACT.Identity, bias=b_col[:, cb : cb + 1])
             u_sb.append(u_block)
 
         s_node = logit_psum.tile([P, K + 1], F32, name="s_node")

@@ -20,7 +20,8 @@ PAIRS = [(k, k + PIECE_SLOTS) for k in range(0, K, PIECE_SLOTS)]
 LAST_PAIR_CUT = PAIRS[:-1] + [(K - 2, K - 1), (K - 1, K)]
 FIRST_PAIR_CUT = [(0, 1), (1, 2)] + PAIRS[1:]
 V_BLOCKS = 2
-V_PARTS = 2
+V_PARTS = 4
+SRC_PARTS = 2
 UNLISTED = float(S - K)
 
 FLOPS = 2 * C * C * H + 2 * C * K * H
@@ -42,7 +43,7 @@ def tile_attributeembeddinglayer_kernel(tc, table, src, v, b, att, offs, out):
         ]
         table_sb = [held.tile([P, S], F32, name=f"table{cb}") for cb in range(NB)]
         offsets = held.tile([P, K * SLOT_COLS], U16, name="offsets")
-        src_for_u = [held.tile([P, NB // V_PARTS, H], BF16, name=f"src_for_u{part}") for part in range(V_PARTS)]
+        src_for_u = [held.tile([P, NB // SRC_PARTS, H], BF16, name=f"src_for_u{part}") for part in range(SRC_PARTS)]
         src_sb = held.tile([P, NB, H], BF16, name="src_sb")
         b_rows = held.tile([NB, P], F32, name="b_rows")
         att_rows = held.tile([NB, P], BF16, name="att_rows")
@@ -50,9 +51,9 @@ def tile_attributeembeddinglayer_kernel(tc, table, src, v, b, att, offs, out):
         nc.sync.dma_start(att_rows[:], att.rearrange("(n p) o -> n (p o)", p=P))
 
         src_by_rows = src.rearrange("(p n) i -> p n i", n=NB)
-        for part in range(V_PARTS):
+        for part in range(SRC_PARTS):
             nc.scalar.dma_start(
-                src_for_u[part][:], src_by_rows[:, part * (NB // V_PARTS) : (part + 1) * (NB // V_PARTS), :]
+                src_for_u[part][:], src_by_rows[:, part * (NB // SRC_PARTS) : (part + 1) * (NB // SRC_PARTS), :]
             )
         for cb in range(NB):
             if cb % V_BLOCKS == 0:
@@ -98,7 +99,7 @@ def tile_attributeembeddinglayer_kernel(tc, table, src, v, b, att, offs, out):
                     lhsT=v_sb[cb // V_BLOCKS][eb // (NB // V_PARTS)][
                         :, eb % (NB // V_PARTS), (cb % V_BLOCKS) * P : (cb % V_BLOCKS + 1) * P
                     ],
-                    rhs=src_for_u[eb // (NB // V_PARTS)][:, eb % (NB // V_PARTS), :],
+                    rhs=src_for_u[eb // (NB // SRC_PARTS)][:, eb % (NB // SRC_PARTS), :],
                     start=(eb == 0),
                     stop=(eb == NB - 1),
                 )

@@ -8,7 +8,6 @@ BF16 = mybir.dt.bfloat16
 U16 = mybir.dt.uint16
 ALU = mybir.AluOpType
 ACT = mybir.ActivationFunctionType
-AXIS_X = mybir.AxisListType.X
 
 P = 128
 C, S, K, H = 1024, 256, 8, 128
@@ -22,7 +21,9 @@ FIRST_PAIR_CUT = [(0, 1), (1, 2)] + PAIRS[1:]
 V_BLOCKS = 2
 V_PARTS = 4
 SRC_PARTS = 2
+WIDE_BLOCKS = 2
 UNLISTED = float(S - K)
+TERMS = K + 1
 
 FLOPS = 2 * C * C * H + 2 * C * K * H
 
@@ -79,8 +80,22 @@ def tile_attributeembeddinglayer_kernel(tc, table, src, v, b, att, offs, out):
         make_identity(nc, ident_f32[:])
         ident_bf = held.tile([P, P], BF16, name="ident_bf")
         make_identity(nc, ident_bf[:])
-        ln_unlisted = held.tile([P, 1], F32, name="ln_unlisted")
-        nc.gpsimd.memset(ln_unlisted[:], math.log(UNLISTED))
+        signs = held.tile([P, K, K, TERMS], BF16, name="signs")
+        nc.vector.memset(signs[:], 0.0)
+        for q in range(K):
+            nc.vector.memset(signs[:, q, :, q : q + 1], 1.0)
+            nc.vector.memset(signs[:, q, q, :], -1.0)
+            nc.vector.memset(signs[:, q, q, q : q + 1], 0.0)
+        sign_rows = held.tile([K, K, TERMS], F32, name="sign_rows")
+        nc.vector.tensor_tensor(
+            sign_rows[:],
+            ident_f32[0:K, 0:TERMS].unsqueeze(1).to_broadcast([K, K, TERMS]),
+            ident_f32[0:K, 0:K].unsqueeze(2).to_broadcast([K, K, TERMS]),
+            ALU.subtract,
+        )
+        ln_unlisted = held.tile([P, K, TERMS], F32, name="ln_unlisted")
+        nc.gpsimd.memset(ln_unlisted[:], 0.0)
+        nc.gpsimd.memset(ln_unlisted[:, :, K : K + 1], math.log(UNLISTED))
 
         columns_ps = block_psum.tile([P, 2 * NB], F32, name="columns_ps", tag="block")
         nc.tensor.matmul(columns_ps[:, 0:NB], lhsT=b_rows[:], rhs=ident_f32[0:NB, 0:NB], start=True, stop=True)
@@ -89,6 +104,13 @@ def tile_attributeembeddinglayer_kernel(tc, table, src, v, b, att, offs, out):
         nc.vector.tensor_copy(b_col[:], columns_ps[:, 0:NB])
         att_col = held.tile([P, NB], BF16, name="att_col")
         nc.vector.tensor_copy(att_col[:], columns_ps[:, NB : 2 * NB])
+        signed_att = {}
+        for cb in range(NB - WIDE_BLOCKS, NB):
+            signed_block = held.tile([P, K, K * TERMS], BF16, name=f"signed_att{cb}")
+            nc.vector.tensor_scalar_mul(
+                signed_block[:], signs[:].rearrange("p q k m -> p q (k m)"), att_col[:, cb : cb + 1]
+            )
+            signed_att[cb] = signed_block
 
         u_sb = []
         for cb in range(NB):
@@ -112,8 +134,12 @@ def tile_attributeembeddinglayer_kernel(tc, table, src, v, b, att, offs, out):
                 nc.scalar.activation(u_copies, u_repeated, ACT.Identity, bias=b_col[:, cb : cb + 1])
             u_sb.append(u_block)
 
-        s_node = logit_psum.tile([P, K + 1], F32, name="s_node")
-        nc.tensor.matmul(s_node[:, K : K + 1], lhsT=ident_f32[:], rhs=ln_unlisted[:], start=True, stop=False)
+        s_sum = logit_psum.tile([P, K], F32, name="s_sum", tag="a_ps6")
+        exponents = logit_psum.tile([P, K, TERMS], F32, name="exponents")
+        exponents_flat = exponents[:].rearrange("p k m -> p (k m)")
+        nc.tensor.matmul(
+            exponents_flat, lhsT=ident_f32[:], rhs=ln_unlisted[:].rearrange("p k m -> p (k m)"), start=True, stop=False
+        )
         for cb in range(NB):
             h = work.tile([P, K * H], BF16, name="h")
             for k0, k1 in LAST_PAIR_CUT if cb == NB - 1 else PAIRS:
@@ -123,25 +149,46 @@ def tile_attributeembeddinglayer_kernel(tc, table, src, v, b, att, offs, out):
                 nc.vector.tensor_tensor(z[:, 0:width], picked, u_sb[cb][:, 0:width], ALU.add)
                 nc.scalar.activation(h[:, k0 * H : k1 * H], z[:, 0:width], ACT.Tanh)
                 for k in range(k0, k1):
-                    nc.tensor.matmul(
-                        s_node[:, k : k + 1],
-                        lhsT=h[:, k * H : (k + 1) * H],
-                        rhs=att_col[:, cb : cb + 1],
-                        start=False,
-                        stop=(cb == NB - 1 and k == K - 1),
-                    )
+                    h_slot = h[:, k * H : (k + 1) * H]
+                    if cb < NB - WIDE_BLOCKS:
+                        nc.tensor.matmul(
+                            s_sum[:, k : k + 1],
+                            lhsT=h_slot,
+                            rhs=att_col[:, cb : cb + 1],
+                            start=(cb == 0 and k == 0),
+                            stop=(cb == NB - WIDE_BLOCKS - 1 and k == K - 1),
+                        )
+                    else:
+                        nc.tensor.matmul(
+                            exponents_flat,
+                            lhsT=h_slot,
+                            rhs=signed_att[cb][:, k, :],
+                            start=False,
+                            stop=(cb == NB - 1 and k == K - 1),
+                        )
+            if cb == NB - 2:
+                s_sum_sb = held.tile([P, K], F32, name="s_sum_sb")
+                nc.scalar.copy(s_sum_sb[:], s_sum[:])
+                s_rows_ps = block_psum.tile([K, P], F32, name="s_rows_ps", tag="block")
+                nc.tensor.transpose(s_rows_ps[:], s_sum_sb[:], ident_f32[:])
+                s_rows = held.tile([K, P], F32, name="s_rows")
+                nc.scalar.copy(s_rows[:], s_rows_ps[:])
+                nc.tensor.matmul(
+                    exponents_flat,
+                    lhsT=s_rows[:],
+                    rhs=sign_rows[:].rearrange("q k m -> q (k m)"),
+                    start=False,
+                    stop=False,
+                )
 
-        neg_shift = held.tile([P, 1], F32, name="neg_shift")
-        nc.vector.tensor_reduce(out=neg_shift[:], in_=s_node[:], axis=AXIS_X, op=ALU.max, negate=True)
-        e_node = held.tile([P, K + 1], F32, name="e_node")
-        denom = held.tile([P, 1], F32, name="denom")
-        nc.scalar.activation(e_node[:], s_node[:], ACT.Exp, bias=neg_shift[:, 0:1], accum_out=denom[:])
-        recip = held.tile([P, 1], F32, name="recip")
-        nc.vector.reciprocal(recip[:], denom[:])
+        terms = held.tile([P, K, TERMS], F32, name="terms")
+        denom = held.tile([P, K], F32, name="denom")
         a_node = held.tile([P, K], F32, name="a_node")
-        nc.vector.tensor_scalar_mul(a_node[:], e_node[:, 0:K], recip[:, 0:1])
         a = held.tile([P, K * H], F32, name="a")
         for k0, k1 in FIRST_PAIR_CUT:
+            for k in range(k0, k1):
+                nc.scalar.activation(terms[:, k, :], exponents[:, k, :], ACT.Exp, accum_out=denom[:, k : k + 1])
+            nc.vector.reciprocal(a_node[:, k0:k1], denom[:, k0:k1])
             a_ps = logit_psum.tile([P, (k1 - k0) * H], F32, name=f"a_ps{k0}")
             for k in range(k0, k1):
                 nc.tensor.transpose(

import math

import concourse.mybir as mybir
from concourse.masks import make_identity

F32 = mybir.dt.float32
BF16 = mybir.dt.bfloat16
U16 = mybir.dt.uint16
ALU = mybir.AluOpType
ACT = mybir.ActivationFunctionType

P = 128
C, S, K, H = 1024, 256, 8, 128
NB = C // P
PIECE_SLOTS = 2
PIECE = PIECE_SLOTS * H
SLOT_COLS = H // 16
PAIRS = [(k, k + PIECE_SLOTS) for k in range(0, K, PIECE_SLOTS)]
LAST_PAIR_CUT = PAIRS[:-1] + [(K - 2, K - 1), (K - 1, K)]
FIRST_PAIR_CUT = [(0, 1), (1, 2)] + PAIRS[1:]
V_BLOCKS = 2
V_PARTS = 4
SRC_PARTS = 2
WIDE_BLOCKS = 2
UNLISTED = float(S - K)
TERMS = K + 1

FLOPS = 2 * C * C * H + 2 * C * K * H


def tile_attributeembeddinglayer_kernel(tc, table, src, v, b, att, offs, out):
    nc = tc.nc
    with (
        tc.tile_pool(name="held", bufs=1) as held,
        tc.tile_pool(name="work", bufs=4) as work,
        tc.tile_pool(name="sums", bufs=12) as sums,
        tc.psum_pool(name="block_psum", bufs=2) as block_psum,
        tc.psum_pool(name="logit_psum", bufs=1) as logit_psum,
    ):
        v_by_rows = v.rearrange("(p n) c -> p n c", n=NB)
        v_sb = [
            [held.tile([P, NB // V_PARTS, V_BLOCKS * P], BF16, name=f"v{g}_{part}") for part in range(V_PARTS)]
            for g in range(NB // V_BLOCKS)
        ]
        table_sb = [held.tile([P, S], F32, name=f"table{cb}") for cb in range(NB)]
        offsets = held.tile([P, K * SLOT_COLS], U16, name="offsets")
        src_for_u = [held.tile([P, NB // SRC_PARTS, H], BF16, name=f"src_for_u{part}") for part in range(SRC_PARTS)]
        src_sb = held.tile([P, NB, H], BF16, name="src_sb")
        b_rows = held.tile([NB, P], F32, name="b_rows")
        att_rows = held.tile([NB, P], BF16, name="att_rows")
        nc.sync.dma_start(b_rows[:], b.rearrange("(n p) o -> n (p o)", p=P))
        nc.sync.dma_start(att_rows[:], att.rearrange("(n p) o -> n (p o)", p=P))

        src_by_rows = src.rearrange("(p n) i -> p n i", n=NB)
        for part in range(SRC_PARTS):
            nc.scalar.dma_start(
                src_for_u[part][:], src_by_rows[:, part * (NB // SRC_PARTS) : (part + 1) * (NB // SRC_PARTS), :]
            )
        for cb in range(NB):
            if cb % V_BLOCKS == 0:
                g = cb // V_BLOCKS
                for part in range(V_PARTS):
                    nc.sync.dma_start(
                        v_sb[g][part][:],
                        v_by_rows[
                            :,
                            part * (NB // V_PARTS) : (part + 1) * (NB // V_PARTS),
                            g * V_BLOCKS * P : (g + 1) * V_BLOCKS * P,
                        ],
                    )
            if cb == 0:
                nc.sync.dma_start(offsets[:], offs)
            nc.sync.dma_start(table_sb[cb][:], table[cb * P : (cb + 1) * P, :])
        nc.sync.dma_start(src_sb[:], src.rearrange("(n p) i -> p n i", p=P))
        warm = held.tile([P, 1], F32, name="warm")
        nc.vector.memset(warm[:], 0.0)
        nc.scalar.activation(warm[:], warm[:], ACT.Tanh)

        ident_f32 = held.tile([P, P], F32, name="ident_f32")
        make_identity(nc, ident_f32[:])
        ident_bf = held.tile([P, P], BF16, name="ident_bf")
        make_identity(nc, ident_bf[:])
        signs = held.tile([P, K, K, TERMS], BF16, name="signs")
        nc.vector.memset(signs[:], 0.0)
        for q in range(K):
            nc.vector.memset(signs[:, q, :, q : q + 1], 1.0)
            nc.vector.memset(signs[:, q, q, :], -1.0)
            nc.vector.memset(signs[:, q, q, q : q + 1], 0.0)
        sign_rows = held.tile([K, K, TERMS], F32, name="sign_rows")
        nc.vector.tensor_tensor(
            sign_rows[:],
            ident_f32[0:K, 0:TERMS].unsqueeze(1).to_broadcast([K, K, TERMS]),
            ident_f32[0:K, 0:K].unsqueeze(2).to_broadcast([K, K, TERMS]),
            ALU.subtract,
        )
        ln_unlisted = held.tile([P, K, TERMS], F32, name="ln_unlisted")
        nc.gpsimd.memset(ln_unlisted[:], 0.0)
        nc.gpsimd.memset(ln_unlisted[:, :, K : K + 1], math.log(UNLISTED))

        columns_ps = block_psum.tile([P, 2 * NB], F32, name="columns_ps", tag="block")
        nc.tensor.matmul(columns_ps[:, 0:NB], lhsT=b_rows[:], rhs=ident_f32[0:NB, 0:NB], start=True, stop=True)
        nc.tensor.matmul(columns_ps[:, NB : 2 * NB], lhsT=att_rows[:], rhs=ident_bf[0:NB, 0:NB], start=True, stop=True)
        b_col = held.tile([P, NB], F32, name="b_col")
        nc.vector.tensor_copy(b_col[:], columns_ps[:, 0:NB])
        att_col = held.tile([P, NB], BF16, name="att_col")
        nc.vector.tensor_copy(att_col[:], columns_ps[:, NB : 2 * NB])
        signed_att = {}
        for cb in range(NB - WIDE_BLOCKS, NB):
            signed_block = held.tile([P, K, K * TERMS], BF16, name=f"signed_att{cb}")
            nc.vector.tensor_scalar_mul(
                signed_block[:], signs[:].rearrange("p q k m -> p q (k m)"), att_col[:, cb : cb + 1]
            )
            signed_att[cb] = signed_block

        u_sb = []
        for cb in range(NB):
            u_ps = block_psum.tile([P, H], F32, name="u_ps", tag="block")
            for eb in range(NB):
                nc.tensor.matmul(
                    u_ps[:],
                    lhsT=v_sb[cb // V_BLOCKS][eb // (NB // V_PARTS)][
                        :, eb % (NB // V_PARTS), (cb % V_BLOCKS) * P : (cb % V_BLOCKS + 1) * P
                    ],
                    rhs=src_for_u[eb // (NB // SRC_PARTS)][:, eb % (NB // SRC_PARTS), :],
                    start=(eb == 0),
                    stop=(eb == NB - 1),
                )
            u_block = held.tile([P, PIECE], F32, name=f"u{cb}")
            u_copies = u_block[:].rearrange("p (t i) -> p t i", t=PIECE_SLOTS)
            u_repeated = u_ps[:].unsqueeze(1).to_broadcast([P, PIECE_SLOTS, H])
            if cb == 0:
                nc.vector.tensor_scalar_add(u_copies, u_repeated, b_col[:, cb : cb + 1])
            else:
                nc.scalar.activation(u_copies, u_repeated, ACT.Identity, bias=b_col[:, cb : cb + 1])
            u_sb.append(u_block)

        s_sum = logit_psum.tile([P, K], F32, name="s_sum", tag="a_ps6")
        exponents = logit_psum.tile([P, K, TERMS], F32, name="exponents")
        exponents_flat = exponents[:].rearrange("p k m -> p (k m)")
        nc.tensor.matmul(
            exponents_flat, lhsT=ident_f32[:], rhs=ln_unlisted[:].rearrange("p k m -> p (k m)"), start=True, stop=False
        )
        for cb in range(NB):
            h = work.tile([P, K * H], BF16, name="h")
            for k0, k1 in LAST_PAIR_CUT if cb == NB - 1 else PAIRS:
                width = (k1 - k0) * H
                z = sums.tile([P, PIECE], F32, name="z")
                picked = table_sb[cb][:].indirect(offsets[:, k0 * SLOT_COLS : k1 * SLOT_COLS])
                nc.vector.tensor_tensor(z[:, 0:width], picked, u_sb[cb][:, 0:width], ALU.add)
                nc.scalar.activation(h[:, k0 * H : k1 * H], z[:, 0:width], ACT.Tanh)
                for k in range(k0, k1):
                    h_slot = h[:, k * H : (k + 1) * H]
                    if cb < NB - WIDE_BLOCKS:
                        nc.tensor.matmul(
                            s_sum[:, k : k + 1],
                            lhsT=h_slot,
                            rhs=att_col[:, cb : cb + 1],
                            start=(cb == 0 and k == 0),
                            stop=(cb == NB - WIDE_BLOCKS - 1 and k == K - 1),
                        )
                    else:
                        nc.tensor.matmul(
                            exponents_flat,
                            lhsT=h_slot,
                            rhs=signed_att[cb][:, k, :],
                            start=False,
                            stop=(cb == NB - 1 and k == K - 1),
                        )
            if cb == NB - 2:
                s_sum_sb = held.tile([P, K], F32, name="s_sum_sb")
                nc.scalar.copy(s_sum_sb[:], s_sum[:])
                s_rows_ps = block_psum.tile([K, P], F32, name="s_rows_ps", tag="block")
                nc.tensor.transpose(s_rows_ps[:], s_sum_sb[:], ident_f32[:])
                s_rows = held.tile([K, P], F32, name="s_rows")
                nc.scalar.copy(s_rows[:], s_rows_ps[:])
                nc.tensor.matmul(
                    exponents_flat,
                    lhsT=s_rows[:],
                    rhs=sign_rows[:].rearrange("q k m -> q (k m)"),
                    start=False,
                    stop=False,
                )

        terms = held.tile([P, K, TERMS], F32, name="terms")
        denom = held.tile([P, K], F32, name="denom")
        a_node = held.tile([P, K], F32, name="a_node")
        a = held.tile([P, K * H], F32, name="a")
        for k0, k1 in FIRST_PAIR_CUT:
            for k in range(k0, k1):
                nc.scalar.activation(terms[:, k, :], exponents[:, k, :], ACT.Exp, accum_out=denom[:, k : k + 1])
            nc.vector.reciprocal(a_node[:, k0:k1], denom[:, k0:k1])
            a_ps = logit_psum.tile([P, (k1 - k0) * H], F32, name=f"a_ps{k0}")
            for k in range(k0, k1):
                nc.tensor.transpose(
                    a_ps[:, (k - k0) * H : (k - k0 + 1) * H], a_node[:, k : k + 1].to_broadcast([P, P]), ident_f32[:]
                )
            if k0 == 0:
                nc.vector.tensor_copy(a[:, k0 * H : k1 * H], a_ps[:])
            else:
                nc.scalar.copy(a[:, k0 * H : k1 * H], a_ps[:])

        for cb in range(NB):
            on_tensor = K - PIECE_SLOTS if cb == NB - 1 else K
            acc = block_psum.tile([P, H], F32, name="acc", tag="block")
            nc.tensor.matmul(acc[:], lhsT=ident_bf[:], rhs=src_sb[:, cb, :], start=True, stop=False)
            for k0, k1 in FIRST_PAIR_CUT if cb == 0 else PAIRS:
                prod = work.tile([P, PIECE], F32, name="prod")
                picked = table_sb[cb][:].indirect(offsets[:, k0 * SLOT_COLS : k1 * SLOT_COLS])
                nc.vector.tensor_tensor(prod[:, 0 : (k1 - k0) * H], picked, a[:, k0 * H : k1 * H], ALU.mult)
                for k in range(k0, min(k1, on_tensor)):
                    nc.tensor.matmul(
                        acc[:],
                        lhsT=ident_f32[:],
                        rhs=prod[:, (k - k0) * H : (k - k0 + 1) * H],
                        start=False,
                        stop=(k == on_tensor - 1),
                    )
            res = work.tile([P, H], F32, name="res")
            if cb == NB - 1:
                pair_sum = work.tile([P, H], F32, name="pair_sum")
                nc.vector.tensor_tensor(pair_sum[:], prod[:, 0:H], prod[:, H : 2 * H], ALU.add)
                nc.vector.tensor_tensor(res[:], acc[:], pair_sum[:], ALU.add)
            else:
                nc.scalar.copy(res[:], acc[:])
            nc.sync.dma_start(out[cb * P : (cb + 1) * P, :], res[:])
